import numpy as np
import ml_dtypes


def mxq(x, axis, fmt="e4m3"):
    dtype, down = {"e4m3": (ml_dtypes.float8_e4m3fn, 7), "e5m2": (ml_dtypes.float8_e5m2, 14)}[fmt]
    v = np.moveaxis(np.asarray(x, np.float32).astype(ml_dtypes.bfloat16).astype(np.float64), axis, -1)
    blocks = v.reshape(v.shape[:-1] + (-1, 32))
    amax = np.abs(blocks).max(-1, keepdims=True)
    byte = np.maximum(np.where(amax > 0, np.frexp(amax)[1] - 1 + 127, 0) - down, 1)
    scale = np.exp2(byte - 127.0)
    codes = (blocks / scale).astype(np.float32).astype(dtype).astype(np.float64)
    return np.moveaxis((codes * scale).reshape(v.shape), -1, axis)


WIDE = False


def mx_kscale(k):
    if not WIDE:
        return np.ones(k)
    levels = np.array([10, -10, 5, -5, 0])
    if k % 512:
        return np.exp2(np.random.permutation(np.resize(levels, k // 32))).repeat(32)
    a = np.empty((k // 512, 16))
    for p in range(k // 512):
        a[p, :8] = np.random.permutation(np.resize(levels, 8))
        for g in range(8):
            far = levels[np.abs(levels - a[p, g]) >= 10]
            a[p, g + 8] = far[np.random.randint(len(far))]
    return np.exp2(a.ravel()).repeat(32)


BF16 = ml_dtypes.bfloat16


def bf(x):
    return np.asarray(x, np.float32).astype(BF16)


def f64(x):
    return np.asarray(x).astype(np.float64)


B, S, DIM, H, NOPE, ROPE_SP, V_SP, KV_RANK = 2, 256, 2048, 16, 64, 128, 128, 512
C = 1.0
QK_SP = NOPE + ROPE_SP


def lift(sp):
    return np.concatenate([np.sqrt((sp * sp).sum(-1, keepdims=True) + C), sp], -1)


def rope(u, cos, sin):
    u1, u2 = u[..., 0::2], u[..., 1::2]
    cos, sin = cos[None, :, None, :], sin[None, :, None, :]
    return np.stack([u1 * cos - u2 * sin, u1 * sin + u2 * cos], -1).reshape(u.shape)


def draw0():
    s = mx_kscale(DIM)
    inv = 1.0 / (10000.0 ** (np.arange(0, ROPE_SP, 2) / ROPE_SP))
    ang = np.arange(S)[:, None] * inv[None, :]
    return {"x": bf(np.random.standard_normal((B, S, DIM)) * s),
            "freqs_cos": bf(np.cos(ang)),
            "freqs_sin": bf(np.sin(ang)),
            "wq_w": bf(np.random.standard_normal((H * QK_SP, DIM)) * 0.3 / np.sqrt(DIM) / s[None, :]),
            "wq_b": bf(np.random.standard_normal(H * QK_SP) * 0.1)}


def core(x, freqs_cos, freqs_sin, wq_w, wq_b):
    q = (mxq(f64(x), 2, "e4m3") @ mxq(f64(wq_w), 1, "e4m3").T) + f64(wq_b)
    q = q.reshape(B, S, H, QK_SP)
    q_nope, q_pe = q[..., :NOPE], q[..., NOPE:]
    q_pe = rope(q_pe, f64(freqs_cos), f64(freqs_sin))
    return lift(np.concatenate([q_nope, q_pe], -1))


def e4m3fn_bytes(y):
    return np.clip(np.asarray(y, np.float64), -448.0, 448.0).astype(np.float32).astype(ml_dtypes.float8_e4m3fn).view(np.uint8)


def e4m3fn_values(b):
    return np.asarray(b, np.uint8).view(ml_dtypes.float8_e4m3fn).astype(np.float64)


def setup_inputs():
    d = draw0()
    x0 = np.asarray(d['wq_w']).astype(np.float64)
    s = (np.max(np.abs(x0), axis=(0,), keepdims=True) / 448.0).astype(np.float32)
    out = {}
    for k, v in d.items():
        if k == 'wq_w':
            out['wq_w_bytes'] = e4m3fn_bytes(x0 / s.astype(np.float64))
            out['wq_w_scale'] = s
        else:
            out[k] = v
    return out


def reference(x, freqs_cos, freqs_sin, wq_w_bytes, wq_w_scale, wq_b):
    return core(x, freqs_cos, freqs_sin, e4m3fn_values(wq_w_bytes) * wq_w_scale.astype(np.float64), wq_b)

@@ -1,0 +1,344 @@
+from contextlib import ExitStack
+
+import concourse.mybir as mybir
+from concourse.masks import make_identity
+
+F32 = mybir.dt.float32
+BF16 = mybir.dt.bfloat16
+U32 = mybir.dt.uint32
+U8 = mybir.dt.uint8
+FP8 = mybir.dt.float8_e4m3fn
+FP8X4 = mybir.dt.float8_e4m3fn_x4
+ALU = mybir.AluOpType
+ACT = mybir.ActivationFunctionType
+
+P = 128
+K = 2048
+PASSES = 4
+TOK = 512
+MT = 4
+HEADS = 16
+HW = 193
+OUTW = HEADS * HW
+NCHUNK = 8
+NROW = 24
+
+FLOPS = 2 * TOK * K * 3072
+
+
+def tile_lorentzmla_pb_kernel(tc, x, freqs_cos, freqs_sin, wq_w_bytes, wq_w_scale, wq_b, out):
+    nc = tc.nc
+    x_v = x.flatten_outer_dims()
+    w_v = wq_w_bytes.rearrange("(i p) k -> p i k", p=P)
+    out_v = out.rearrange("b (st p) h c -> p (b st) (h c)", p=P)
+    scale_row = wq_w_scale.rearrange("o k -> (o k)")
+
+    with ExitStack() as ctx:
+        const = ctx.enter_context(tc.tile_pool(name="const", bufs=1))
+        wbp = ctx.enter_context(tc.tile_pool(name="wbp", bufs=6))
+        xsp = ctx.enter_context(tc.tile_pool(name="xsp", bufs=4))
+        wbfp = ctx.enter_context(tc.tile_pool(name="wbfp", bufs=4))
+        wgp = ctx.enter_context(tc.tile_pool(name="wgp", bufs=2))
+        wcp = ctx.enter_context(tc.tile_pool(name="wcp", bufs=2))
+        up = ctx.enter_context(tc.tile_pool(name="up", bufs=4))
+        qnp = ctx.enter_context(tc.tile_pool(name="qnp", bufs=2))
+        tpp = ctx.enter_context(tc.psum_pool(name="tpp", bufs=2))
+        accp = ctx.enter_context(tc.psum_pool(name="accp", bufs=4))
+        finp = ctx.enter_context(tc.psum_pool(name="finp", bufs=2))
+        ctx.enter_context(tc.manual_schedule(engines={mybir.EngineType.PE}))
+
+        scale_bc = const.tile([P, K], F32, name="scale_bc")
+        wbytes = {}
+        xs = {}
+
+        def new_w(a):
+            wbytes[a] = wbp.tile([P, 3, K], U8, name="wbytes", tag="wbytes")
+
+        def load_w_row(a, j):
+            nc.sync.dma_start(out=wbytes[a][:, j, :], in_=w_v[:, 3 * a + j, :])
+
+        def load_x(m):
+            xs[m] = xsp.tile([P, K], BF16, name="xs", tag="xs")
+            nc.sync.dma_start(out=xs[m][:], in_=x_v[m * P : (m + 1) * P, :])
+
+        new_w(0)
+        new_w(1)
+        srow = const.tile([P, P], F32, name="srow")
+        nc.gpsimd.memset(srow[:], 0.0)
+        nc.sync.dma_start(out=srow[0:16, :], in_=scale_row.rearrange("(c p) -> c p", p=P))
+        load_w_row(0, 0)
+        load_w_row(0, 1)
+        load_w_row(0, 2)
+        load_x(0)
+        load_x(1)
+        load_w_row(1, 0)
+        load_x(2)
+        load_w_row(1, 1)
+        load_x(3)
+        load_w_row(1, 2)
+        for a in range(2, NCHUNK):
+            new_w(a)
+            nc.sync.dma_start(out=wbytes[a][:], in_=w_v[:, 3 * a : 3 * a + 3, :])
+
+        cos_raw = const.tile([P, 2, 64], BF16, name="cos_raw")
+        sin_raw = const.tile([P, 2, 64], BF16, name="sin_raw")
+        nc.scalar.dma_start(out=cos_raw[:], in_=freqs_cos.rearrange("(st p) j -> p st j", p=P))
+        nc.scalar.dma_start(out=sin_raw[:], in_=freqs_sin.rearrange("(st p) j -> p st j", p=P))
+        braw = const.tile([P, P], BF16, name="braw")
+        nc.gpsimd.memset(braw[:], 0.0)
+        warm = const.tile([P, 1], F32, name="warm")
+        nc.gpsimd.memset(warm[:], 1.0)
+        nc.scalar.dma_start(out=braw[0:16, :], in_=wq_b.rearrange("(h c) -> h c", c=192)[:, 64:192])
+        nc.scalar.dma_start(
+            out=braw[16:24, :].rearrange("a (f c) -> a f c", f=2),
+            in_=wq_b.rearrange("(a f c) -> a f c", f=2, c=192)[:, :, 0:64],
+        )
+
+        warm2 = const.tile([P, 1], F32, name="warm2")
+        nc.scalar.activation(out=warm2[:], in_=warm[:], func=ACT.Sqrt)
+
+        ident_f = const.tile([P, P], F32, name="ident_f")
+        make_identity(nc, ident_f[:])
+        tps = tpp.tile([P, P], F32, name="tps", tag="tp")
+        nc.tensor.transpose(tps[:], srow[:], ident_f[:])
+        scale_col = const.tile([P, 16], F32, name="scale_col")
+        nc.vector.tensor_copy(out=scale_col[:], in_=tps[:, 0:16])
+        for q in range(4):
+            psb = accp.tile([P, 4, P], F32, name="psb", tag="acc")
+            for c in range(4):
+                col = 4 * q + c
+                nc.tensor.transpose(psb[:, c, :], scale_col[:, col : col + 1].to_broadcast([P, P]), ident_f[:])
+            nc.scalar.copy(out=scale_bc[:, 512 * q : 512 * (q + 1)], in_=psb[:].rearrange("p c n -> p (c n)"))
+        ident_b = const.tile([P, P], BF16, name="ident_b")
+        make_identity(nc, ident_b[:])
+        swapm = const.tile([P, 64, 2], F32, name="swapm")
+        idv = ident_f[:].rearrange("p (j e) -> p j e", e=2)
+        nc.scalar.copy(out=swapm[:, :, 0], in_=idv[:, :, 1])
+        nc.scalar.copy(out=swapm[:, :, 1], in_=idv[:, :, 0])
+        swap2 = swapm[:].rearrange("p j e -> p (j e)")
+
+        c_il = const.tile([P, 2, 64, 2], BF16, name="c_il")
+        s_il = const.tile([P, 2, 64, 2], BF16, name="s_il")
+        nc.scalar.copy(out=c_il[:, :, :, 0], in_=cos_raw[:])
+        nc.scalar.copy(out=c_il[:, :, :, 1], in_=cos_raw[:])
+        nc.scalar.copy(out=s_il[:, :, :, 0], in_=sin_raw[:])
+        nc.scalar.mul(out=s_il[:, :, :, 1], in_=sin_raw[:], mul=-1.0)
+
+        tpt = tpp.tile([P, 4, P], BF16, name="tpt", tag="tp")
+        for st in range(2):
+            nc.tensor.transpose(tpt[:, st, :], c_il[:, st, :, :].rearrange("p j e -> p (j e)"), ident_b[:])
+            nc.tensor.transpose(tpt[:, 2 + st, :], s_il[:, st, :, :].rearrange("p j e -> p (j e)"), ident_b[:])
+        cos_t = const.tile([P, 2, 256], F32, name="cos_t")
+        sin_t = const.tile([P, 2, 256], F32, name="sin_t")
+        for b in range(2):
+            nc.scalar.copy(out=cos_t[:, b, :], in_=tpt[:, 0:2, :].rearrange("p s r -> p (s r)"))
+            nc.scalar.copy(out=sin_t[:, b, :], in_=tpt[:, 2:4, :].rearrange("p s r -> p (s r)"))
+        cos_f = cos_t[:].rearrange("p b s -> p (b s)")
+        sin_f = sin_t[:].rearrange("p b s -> p (b s)")
+
+        tpb = tpp.tile([P, P], BF16, name="tpb", tag="tp")
+        nc.tensor.transpose(tpb[:], braw[:], ident_b[:])
+        bias_col = const.tile([P, 24], F32, name="bias_col")
+        nc.scalar.copy(out=bias_col[:], in_=tpb[:, 0:24])
+
+        x_codes = const.tile([P, PASSES, TOK], U32, name="x_codes", align_bytes=64)
+        x_scales = const.tile([P, PASSES, TOK], U8, name="x_scales", align_bytes=64)
+        xg = const.tile([P, PASSES, TOK, 4], BF16, name="xg", align_bytes=64)
+        o_sb = const.tile([P, MT, OUTW], F32, name="o_sb")
+        o4 = o_sb[:].rearrange("p m (h c) -> p m h c", c=HW)
+        ssum = const.tile([P, MT, HEADS], F32, name="ssum")
+
+        def word_transposes(src, gp):
+            words = src[:].bitcast(F32)
+            tp = tpp.tile([P, 2, 2, P], F32, name="tp", tag="tp")
+            for g2 in range(2):
+                g = 2 * gp + g2
+                for u in range(2):
+                    nc.tensor.transpose(tp[:, g2, u, :], words[:, 256 * g + u : 256 * (g + 1) : 2], ident_f[:])
+            return tp
+
+        wbf = {}
+        wg = {}
+        wc = {}
+        acc = {}
+        post = {}
+        fins = {}
+
+        def st_tt(r):
+            a, j = divmod(r, 3)
+            t = wbfp.tile([P, K], BF16, name="wbf", tag="wbf")
+            pieces = 4 if r == 0 else 1
+            w = K // pieces
+            for q in range(pieces):
+                qs = slice(q * w, (q + 1) * w)
+                nc.vector.tensor_tensor(out=t[:, qs], in0=wbytes[a][:, j, qs].bitcast(FP8), in1=scale_bc[:, qs], op=ALU.mult)
+            wbf[r] = t
+
+        def wt_half(r, gp):
+            a, j = divmod(r, 3)
+            if j == 0 and gp == 0:
+                wg[(a, 0)] = wgp.tile([P, 2, PASSES, P, 4], BF16, name="wga", tag="wga", align_bytes=64)
+            if j == 2 and gp == 0:
+                wg[(a, 1)] = wgp.tile([P, 1, PASSES, P, 4], BF16, name="wgb", tag="wgb", align_bytes=64)
+            tp = word_transposes(wbf[r], gp)
+            gs = slice(2 * gp, 2 * gp + 2)
+            if j == 2:
+                dst = wg[(a, 1)][:].bitcast(F32)
+                nc.scalar.copy(out=dst[:, 0, gs, :, :], in_=tp[:].rearrange("p g u r -> p g r u"))
+            else:
+                dst = wg[(a, 0)][:].bitcast(F32)
+                for hf in range(2):
+                    unit = hf if j == 0 else 1 - hf
+                    nc.scalar.copy(
+                        out=dst[:, unit, gs, 64 * j : 64 * j + 64, :],
+                        in_=tp[:, :, :, 64 * hf : 64 * hf + 64].rearrange("p g u r -> p g r u"),
+                    )
+
+        def st_quant(a, grp):
+            n = 2 if grp == 0 else 1
+            cod = wcp.tile([P, n, PASSES, P], U32, name="wcod%d" % grp, tag="wcod%d" % grp, align_bytes=64)
+            sca = wcp.tile([P, n, PASSES, P], U8, name="wsca%d" % grp, tag="wsca%d" % grp, align_bytes=64)
+            nc.vector.quantize_mx(
+                out=cod[:].rearrange("p n g c -> p (n g c)").bitcast(FP8X4),
+                scales=sca[:].rearrange("p n g c -> p (n g c)"),
+                in_=wg[(a, grp)][:].rearrange("p n g c t -> p (n g c t)"),
+            )
+            wc[(a, grp)] = (cod, sca)
+
+        def unit_info(t):
+            a, i = divmod(t, 3)
+            if i == 0:
+                return (False, a, 0, 0, 16 + a)
+            if i == 1:
+                return (True, 2 * a, 0, 1, 2 * a)
+            return (True, 2 * a + 1, 1, 0, 2 * a + 1)
+
+        def mx_half(t, half):
+            rot, idx, grp, n, bcol = unit_info(t)
+            cod, sca = wc[(t // 3, grp)]
+            if half == 0:
+                acc[t] = accp.tile([P, TOK], F32, name="acc", tag="acc")
+            for g in (2 * half, 2 * half + 1):
+                nc.tensor.matmul_mx(
+                    out=acc[t][:],
+                    lhsT=cod[:, n, g, :].bitcast(FP8X4),
+                    lhsT_scale=sca[:, n, g, :],
+                    rhs=x_codes[:, g, :].bitcast(FP8X4),
+                    rhs_scale=x_scales[:, g, :],
+                    start=(g == 0),
+                    stop=(g == PASSES - 1),
+                )
+
+        def st_post(t):
+            rot, idx, grp, n, bcol = unit_info(t)
+            b_ap = bias_col[:, bcol : bcol + 1]
+            if rot:
+                u1 = up.tile([P, TOK], F32, name="u1", tag="u1")
+                u2 = up.tile([P, TOK], F32, name="u2", tag="u2")
+                nc.vector.scalar_tensor_tensor(out=u1[:], in0=acc[t][:], scalar=b_ap, in1=cos_f, op0=ALU.add, op1=ALU.mult)
+                nc.vector.scalar_tensor_tensor(out=u2[:], in0=acc[t][:], scalar=b_ap, in1=sin_f, op0=ALU.add, op1=ALU.mult)
+                post[t] = (u1, u2)
+            else:
+                qn = qnp.tile([P, TOK], F32, name="qn", tag="qn")
+                nc.scalar.activation(out=qn[:], in_=acc[t][:], func=ACT.Identity, bias=b_ap, scale=1.0)
+                post[t] = (qn,)
+
+        def back_half(t, half):
+            rot, idx, grp, n, bcol = unit_info(t)
+            if half == 0:
+                fins[t] = finp.tile([P, MT, P], F32, name="fin", tag="fin")
+            fin = fins[t]
+            src = post[t]
+            for m in (2 * half, 2 * half + 1):
+                ms = slice(m * P, (m + 1) * P)
+                if rot:
+                    nc.tensor.matmul(fin[:, m, :], lhsT=src[0][:, ms], rhs=ident_f[:], is_transpose=True, start=True, stop=False)
+                    nc.tensor.matmul(fin[:, m, :], lhsT=src[1][:, ms], rhs=swap2, is_transpose=True, start=False, stop=True)
+                else:
+                    nc.tensor.transpose(fin[:, m, :], src[0][:, ms], ident_f[:])
+            if half == 1:
+                if rot:
+                    nc.scalar.copy(out=o4[:, :, idx, 65:193], in_=fin[:])
+                else:
+                    nc.scalar.copy(
+                        out=o4[:, :, 2 * idx : 2 * idx + 2, 1:65],
+                        in_=fin[:].rearrange("p m (f c) -> p m f c", f=2),
+                    )
+
+        def squares(h, on_vector):
+            for m in range(MT):
+                q_ap = o4[:, m, h, 1:193]
+                s_ap = ssum[:, m, h : h + 1]
+                if m in on_vector:
+                    junkv = qnp.tile([P, 192], F32, name="junkv", tag="junkv")
+                    nc.vector.scalar_tensor_tensor(out=junkv[:], in0=q_ap, scalar=1.0, in1=q_ap, op0=ALU.mult, op1=ALU.mult, accum_out=s_ap)
+                else:
+                    junk = qnp.tile([P, 192], F32, name="junk", tag="junk")
+                    nc.scalar.activation(out=junk[:], in_=q_ap, func=ACT.Square, accum_out=s_ap)
+
+        def finish(h0, h1):
+            nc.scalar.activation(out=o4[:, :, h0:h1, 0], in_=ssum[:, :, h0:h1], func=ACT.Sqrt, bias=1.0, scale=1.0)
+            c0 = (h0 * HW) // 8 * 8
+            c1 = (h1 * HW) // 8 * 8
+            nc.sync.dma_start(out=out_v[:, :, c0:c1], in_=o_sb[:, :, c0:c1])
+
+        def st_tail(t):
+            rot, h, grp, n, bcol = unit_info(t)
+            if not rot:
+                return
+            last = t // 3 == NCHUNK - 1
+            squares(h, (2, 3) if t == NROW - 1 else ())
+            if last:
+                finish(h, h + 1)
+            elif grp == 1:
+                finish(h - 1, h + 1)
+
+        def x_transposes(m):
+            xgw = xg[:].bitcast(F32)
+            for gp in range(2):
+                tp = word_transposes(xs[m], gp)
+                nc.scalar.copy(
+                    out=xgw[:, 2 * gp : 2 * gp + 2, m * P : (m + 1) * P, :],
+                    in_=tp[:].rearrange("p g u r -> p g r u"),
+                )
+
+        def x_quant():
+            for g in range(PASSES):
+                nc.vector.quantize_mx(
+                    out=x_codes[:, g, :].bitcast(FP8X4),
+                    scales=x_scales[:, g, :],
+                    in_=xg[:, g, :, :].rearrange("p n t -> p (n t)"),
+                )
+
+        def group_of(r):
+            a, j = divmod(r, 3)
+            if r < 0 or r >= NROW or j == 0:
+                return None
+            return (a, j - 1)
+
+        x_at = {1: (0,), 2: (1,), 3: (2, 3)}
+        for s in range(NROW + 6 + 1):
+            t = s - 5
+            if 0 <= t < NROW and unit_info(t)[0]:
+                st_post(t)
+            t = s - 5
+            if 0 <= t < NROW and not unit_info(t)[0]:
+                st_post(t)
+            g = group_of(s - 2)
+            if g is not None:
+                st_quant(g[0], g[1])
+            if s == 4:
+                x_quant()
+            if s < NROW:
+                st_tt(s)
+            for half in range(2):
+                if 0 <= s - 1 < NROW:
+                    wt_half(s - 1, half)
+                if 0 <= s - 4 < NROW:
+                    mx_half(s - 4, half)
+                if 0 <= s - 6 < NROW:
+                    back_half(s - 6, half)
+            for m in x_at.get(s, ()):
+                x_transposes(m)
+            if 0 <= s - 6 < NROW:
+                st_tail(s - 6)

@@ -128,13 +128,11 @@ def tile_lorentzmla_pb_kernel(tc, x, freqs_cos, freqs_sin, wq_w_bytes, wq_w_scal
         for st in range(2):
             nc.tensor.transpose(tpt[:, st, :], c_il[:, st, :, :].rearrange("p j e -> p (j e)"), ident_b[:])
             nc.tensor.transpose(tpt[:, 2 + st, :], s_il[:, st, :, :].rearrange("p j e -> p (j e)"), ident_b[:])
-        cos_t = const.tile([P, 2, 256], F32, name="cos_t")
-        sin_t = const.tile([P, 2, 256], F32, name="sin_t")
+        cs_t = const.tile([P, 2, 2, 256], F32, name="cs_t")
         for b in range(2):
-            nc.scalar.copy(out=cos_t[:, b, :], in_=tpt[:, 0:2, :].rearrange("p s r -> p (s r)"))
-            nc.scalar.copy(out=sin_t[:, b, :], in_=tpt[:, 2:4, :].rearrange("p s r -> p (s r)"))
-        cos_f = cos_t[:].rearrange("p b s -> p (b s)")
-        sin_f = sin_t[:].rearrange("p b s -> p (b s)")
+            nc.scalar.copy(out=cs_t[:, 0, b, :], in_=tpt[:, 0:2, :].rearrange("p s r -> p (s r)"))
+            nc.scalar.copy(out=cs_t[:, 1, b, :], in_=tpt[:, 2:4, :].rearrange("p s r -> p (s r)"))
+        cs_f = cs_t[:].rearrange("p k b s -> p k (b s)")
 
         tpb = tpp.tile([P, P], BF16, name="tpb", tag="tp")
         nc.tensor.transpose(tpb[:], braw[:], ident_b[:])
@@ -233,15 +231,15 @@ def tile_lorentzmla_pb_kernel(tc, x, freqs_cos, freqs_sin, wq_w_bytes, wq_w_scal
             rot, idx, grp, n, bcol = unit_info(t)
             b_ap = bias_col[:, bcol : bcol + 1]
             if rot:
-                u1 = up.tile([P, TOK], F32, name="u1", tag="u1")
-                u2 = up.tile([P, TOK], F32, name="u2", tag="u2")
-                nc.vector.scalar_tensor_tensor(out=u1[:], in0=acc[t][:], scalar=b_ap, in1=cos_f, op0=ALU.add, op1=ALU.mult)
-                nc.vector.scalar_tensor_tensor(out=u2[:], in0=acc[t][:], scalar=b_ap, in1=sin_f, op0=ALU.add, op1=ALU.mult)
-                post[t] = (u1, u2)
+                u = up.tile([P, 2, TOK], F32, name="u", tag="u")
+                nc.vector.scalar_tensor_tensor(
+                    out=u[:], in0=acc[t][:].unsqueeze(1).to_broadcast([P, 2, TOK]), scalar=b_ap, in1=cs_f, op0=ALU.add, op1=ALU.mult
+                )
+                post[t] = (u[:, 0, :], u[:, 1, :])
             else:
                 qn = qnp.tile([P, TOK], F32, name="qn", tag="qn")
                 nc.scalar.activation(out=qn[:], in_=acc[t][:], func=ACT.Identity, bias=b_ap, scale=1.0)
-                post[t] = (qn,)
+                post[t] = (qn[:],)
 
         def back_half(t, half):
             rot, idx, grp, n, bcol = unit_info(t)

@@ -22,6 +22,7 @@ HW = 193
 OUTW = HEADS * HW
 NCHUNK = 8
 NROW = 24
+NWARM = 3
 
 FLOPS = 2 * TOK * K * 3072
 
@@ -65,6 +66,8 @@ def tile_lorentzmla_pb_kernel(tc, x, freqs_cos, freqs_sin, wq_w_bytes, wq_w_scal
         new_w(1)
         srow = const.tile([P, P], F32, name="srow")
         nc.gpsimd.memset(srow[:], 0.0)
+        wones = const.tile([P, 512], BF16, name="wones")
+        nc.gpsimd.memset(wones[:], 1.0)
         nc.sync.dma_start(out=srow[0:16, :], in_=scale_row.rearrange("(c p) -> c p", p=P))
         load_w_row(0, 0)
         load_w_row(0, 1)
@@ -93,6 +96,10 @@ def tile_lorentzmla_pb_kernel(tc, x, freqs_cos, freqs_sin, wq_w_bytes, wq_w_scal
             out=braw[16:24, :].rearrange("a (f c) -> a f c", f=2),
             in_=wq_b.rearrange("(a f c) -> a f c", f=2, c=192)[:, :, 0:64],
         )
+
+        for i in range(NWARM):
+            wps = finp.tile([P, 512], F32, name="wps", tag="fin")
+            nc.tensor.matmul(wps[:], lhsT=wones[:, 0:P], rhs=wones[:], start=True, stop=True)
 
         warm2 = const.tile([P, 1], F32, name="warm2")
         nc.scalar.activation(out=warm2[:], in_=warm[:], func=ACT.Sqrt)
@@ -332,8 +339,10 @@ def tile_lorentzmla_pb_kernel(tc, x, freqs_cos, freqs_sin, wq_w_bytes, wq_w_scal
             for half in range(2):
                 if 0 <= s - 1 < NROW:
                     wt_half(s - 1, half)
+            for half in range(2):
                 if 0 <= s - 4 < NROW:
                     mx_half(s - 4, half)
+            for half in range(2):
                 if 0 <= s - 6 < NROW:
                     back_half(s - 6, half)
             for m in x_at.get(s, ()):

@@ -337,11 +337,11 @@ def tile_lorentzmla_pb_kernel(tc, x, freqs_cos, freqs_sin, wq_w_bytes, wq_w_scal
             if s < NROW:
                 st_tt(s)
             for half in range(2):
-                if 0 <= s - 1 < NROW:
-                    wt_half(s - 1, half)
-            for half in range(2):
                 if 0 <= s - 4 < NROW:
                     mx_half(s - 4, half)
+            for half in range(2):
+                if 0 <= s - 1 < NROW:
+                    wt_half(s - 1, half)
             for half in range(2):
                 if 0 <= s - 6 < NROW:
                     back_half(s - 6, half)

@@ -43,8 +43,8 @@ def tile_lorentzmla_pb_kernel(tc, x, freqs_cos, freqs_sin, wq_w_bytes, wq_w_scal
         wcp = ctx.enter_context(tc.tile_pool(name="wcp", bufs=2))
         up = ctx.enter_context(tc.tile_pool(name="up", bufs=4))
         qnp = ctx.enter_context(tc.tile_pool(name="qnp", bufs=2))
-        tpp = ctx.enter_context(tc.psum_pool(name="tpp", bufs=2))
-        accp = ctx.enter_context(tc.psum_pool(name="accp", bufs=4))
+        tpp = ctx.enter_context(tc.psum_pool(name="tpp", bufs=3))
+        accp = ctx.enter_context(tc.psum_pool(name="accp", bufs=3))
         finp = ctx.enter_context(tc.psum_pool(name="finp", bufs=2))
         ctx.enter_context(tc.manual_schedule(engines={mybir.EngineType.PE}))
 

@@ -123,6 +123,9 @@ def tile_lorentzmla_pb_kernel(tc, x, freqs_cos, freqs_sin, wq_w_bytes, wq_w_scal
         nc.scalar.copy(out=swapm[:, :, 0], in_=idv[:, :, 1])
         nc.scalar.copy(out=swapm[:, :, 1], in_=idv[:, :, 0])
         swap2 = swapm[:].rearrange("p j e -> p (j e)")
+        rot64 = const.tile([P, P], F32, name="rot64")
+        nc.scalar.copy(out=rot64[:, 0:64], in_=ident_f[:, 64:128])
+        nc.scalar.copy(out=rot64[:, 64:128], in_=ident_f[:, 0:64])
 
         c_il = const.tile([P, 2, 64, 2], BF16, name="c_il")
         s_il = const.tile([P, 2, 64, 2], BF16, name="s_il")
@@ -153,13 +156,13 @@ def tile_lorentzmla_pb_kernel(tc, x, freqs_cos, freqs_sin, wq_w_bytes, wq_w_scal
         o4 = o_sb[:].rearrange("p m (h c) -> p m h c", c=HW)
         ssum = const.tile([P, MT, HEADS], F32, name="ssum")
 
-        def word_transposes(src, gp):
+        def word_transposes(src, gp, perm):
             words = src[:].bitcast(F32)
             tp = tpp.tile([P, 2, 2, P], F32, name="tp", tag="tp")
             for g2 in range(2):
                 g = 2 * gp + g2
                 for u in range(2):
-                    nc.tensor.transpose(tp[:, g2, u, :], words[:, 256 * g + u : 256 * (g + 1) : 2], ident_f[:])
+                    nc.tensor.transpose(tp[:, u, g2, :], words[:, 256 * g + u : 256 * (g + 1) : 2], perm)
             return tp
 
         wbf = {}
@@ -182,31 +185,29 @@ def tile_lorentzmla_pb_kernel(tc, x, freqs_cos, freqs_sin, wq_w_bytes, wq_w_scal
         def wt_half(r, gp):
             a, j = divmod(r, 3)
             if j == 0 and gp == 0:
-                wg[(a, 0)] = wgp.tile([P, 2, PASSES, P, 4], BF16, name="wga", tag="wga", align_bytes=64)
+                wg[(a, 0)] = wgp.tile([P, PASSES, 2, P, 4], BF16, name="wga", tag="wga", align_bytes=64)
             if j == 2 and gp == 0:
-                wg[(a, 1)] = wgp.tile([P, 1, PASSES, P, 4], BF16, name="wgb", tag="wgb", align_bytes=64)
-            tp = word_transposes(wbf[r], gp)
+                wg[(a, 1)] = wgp.tile([P, PASSES, 1, P, 4], BF16, name="wgb", tag="wgb", align_bytes=64)
+            tp = word_transposes(wbf[r], gp, rot64[:] if j == 1 else ident_f[:])
             gs = slice(2 * gp, 2 * gp + 2)
             if j == 2:
                 dst = wg[(a, 1)][:].bitcast(F32)
-                nc.scalar.copy(out=dst[:, 0, gs, :, :], in_=tp[:].rearrange("p g u r -> p g r u"))
+                nc.scalar.copy(out=dst[:, gs, 0, :, :], in_=tp[:].rearrange("p u g r -> p g r u"))
             else:
-                dst = wg[(a, 0)][:].bitcast(F32)
-                for hf in range(2):
-                    unit = hf if j == 0 else 1 - hf
-                    nc.scalar.copy(
-                        out=dst[:, unit, gs, 64 * j : 64 * j + 64, :],
-                        in_=tp[:, :, :, 64 * hf : 64 * hf + 64].rearrange("p g u r -> p g r u"),
-                    )
+                dst = wg[(a, 0)][:].bitcast(F32).rearrange("p g n c u -> p (g n) c u")
+                nc.scalar.copy(
+                    out=dst[:, 4 * gp : 4 * gp + 4, 64 * j : 64 * j + 64, :],
+                    in_=tp[:].rearrange("p u g (n r) -> p (g n) r u", n=2),
+                )
 
         def st_quant(a, grp):
             n = 2 if grp == 0 else 1
-            cod = wcp.tile([P, n, PASSES, P], U32, name="wcod%d" % grp, tag="wcod%d" % grp, align_bytes=64)
-            sca = wcp.tile([P, n, PASSES, P], U8, name="wsca%d" % grp, tag="wsca%d" % grp, align_bytes=64)
+            cod = wcp.tile([P, PASSES, n, P], U32, name="wcod%d" % grp, tag="wcod%d" % grp, align_bytes=64)
+            sca = wcp.tile([P, PASSES, n, P], U8, name="wsca%d" % grp, tag="wsca%d" % grp, align_bytes=64)
             nc.vector.quantize_mx(
-                out=cod[:].rearrange("p n g c -> p (n g c)").bitcast(FP8X4),
-                scales=sca[:].rearrange("p n g c -> p (n g c)"),
-                in_=wg[(a, grp)][:].rearrange("p n g c t -> p (n g c t)"),
+                out=cod[:].rearrange("p g n c -> p (g n c)").bitcast(FP8X4),
+                scales=sca[:].rearrange("p g n c -> p (g n c)"),
+                in_=wg[(a, grp)][:].rearrange("p g n c t -> p (g n c t)"),
             )
             wc[(a, grp)] = (cod, sca)
 
@@ -226,8 +227,8 @@ def tile_lorentzmla_pb_kernel(tc, x, freqs_cos, freqs_sin, wq_w_bytes, wq_w_scal
             for g in (2 * half, 2 * half + 1):
                 nc.tensor.matmul_mx(
                     out=acc[t][:],
-                    lhsT=cod[:, n, g, :].bitcast(FP8X4),
-                    lhsT_scale=sca[:, n, g, :],
+                    lhsT=cod[:, g, n, :].bitcast(FP8X4),
+                    lhsT_scale=sca[:, g, n, :],
                     rhs=x_codes[:, g, :].bitcast(FP8X4),
                     rhs_scale=x_scales[:, g, :],
                     start=(g == 0),
@@ -301,10 +302,10 @@ def tile_lorentzmla_pb_kernel(tc, x, freqs_cos, freqs_sin, wq_w_bytes, wq_w_scal
         def x_transposes(m):
             xgw = xg[:].bitcast(F32)
             for gp in range(2):
-                tp = word_transposes(xs[m], gp)
+                tp = word_transposes(xs[m], gp, ident_f[:])
                 nc.scalar.copy(
                     out=xgw[:, 2 * gp : 2 * gp + 2, m * P : (m + 1) * P, :],
-                    in_=tp[:].rearrange("p g u r -> p g r u"),
+                    in_=tp[:].rearrange("p u g r -> p g r u"),
                 )
 
         def x_quant():

@@ -240,17 +240,40 @@ def tile_lorentzmla_pb_kernel(tc, x, freqs_cos, freqs_sin, wq_w_bytes, wq_w_scal
             b_ap = bias_col[:, bcol : bcol + 1]
             if rot:
                 u = up.tile([P, 2, TOK], F32, name="u", tag="u")
-                nc.vector.scalar_tensor_tensor(
-                    out=u[:], in0=acc[t][:].unsqueeze(1).to_broadcast([P, 2, TOK]), scalar=b_ap, in1=cs_f, op0=ALU.add, op1=ALU.mult
-                )
+                pieces = MT if t == NROW - 1 else 1
+                w = TOK // pieces
+                for q in range(pieces):
+                    qs = slice(q * w, (q + 1) * w)
+                    nc.vector.scalar_tensor_tensor(
+                        out=u[:, :, qs],
+                        in0=acc[t][:, qs].unsqueeze(1).to_broadcast([P, 2, w]),
+                        scalar=b_ap,
+                        in1=cs_f[:, :, qs],
+                        op0=ALU.add,
+                        op1=ALU.mult,
+                    )
                 post[t] = (u[:, 0, :], u[:, 1, :])
             else:
                 qn = qnp.tile([P, TOK], F32, name="qn", tag="qn")
                 nc.scalar.activation(out=qn[:], in_=acc[t][:], func=ACT.Identity, bias=b_ap, scale=1.0)
                 post[t] = (qn[:],)
 
+        def back_last(t):
+            rot, idx, grp, n, bcol = unit_info(t)
+            src = post[t]
+            for m in range(MT):
+                ms = slice(m * P, (m + 1) * P)
+                finq = tpp.tile([P, P], F32, name="finq", tag="tp")
+                nc.tensor.matmul(finq[:], lhsT=src[0][:, ms], rhs=ident_f[:], is_transpose=True, start=True, stop=False)
+                nc.tensor.matmul(finq[:], lhsT=src[1][:, ms], rhs=swap2, is_transpose=True, start=False, stop=True)
+                nc.scalar.copy(out=o4[:, m, idx, 65:193], in_=finq[:])
+
         def back_half(t, half):
             rot, idx, grp, n, bcol = unit_info(t)
+            if t == NROW - 1:
+                if half == 0:
+                    back_last(t)
+                return
             if half == 0:
                 fins[t] = finp.tile([P, MT, P], F32, name="fin", tag="fin")
             fin = fins[t]
@@ -293,7 +316,7 @@ def tile_lorentzmla_pb_kernel(tc, x, freqs_cos, freqs_sin, wq_w_bytes, wq_w_scal
             if not rot:
                 return
             last = t // 3 == NCHUNK - 1
-            squares(h, (2, 3) if t == NROW - 1 else ())
+            squares(h, (0, 1, 2) if t == NROW - 1 else ())
             if last:
                 finish(h, h + 1)
             elif grp == 1:

@@ -64,11 +64,12 @@ def tile_lorentzmla_pb_kernel(tc, x, freqs_cos, freqs_sin, wq_w_bytes, wq_w_scal
 
         new_w(0)
         new_w(1)
-        srow = const.tile([P, P], F32, name="srow")
-        nc.gpsimd.memset(srow[:], 0.0)
+        scale_col = const.tile([P, 16], F32, name="scale_col")
         wones = const.tile([P, 512], BF16, name="wones")
         nc.gpsimd.memset(wones[:], 1.0)
-        nc.sync.dma_start(out=srow[0:16, :], in_=scale_row.rearrange("(c p) -> c p", p=P))
+        nc.sync.dma_start(
+            out=scale_col[:].rearrange("p (g t) -> p g t", t=4), in_=scale_row.rearrange("(g p t) -> p g t", p=P, t=4)
+        )
         load_w_row(0, 0)
         load_w_row(0, 1)
         load_w_row(0, 2)
@@ -106,16 +107,14 @@ def tile_lorentzmla_pb_kernel(tc, x, freqs_cos, freqs_sin, wq_w_bytes, wq_w_scal
 
         ident_f = const.tile([P, P], F32, name="ident_f")
         make_identity(nc, ident_f[:])
-        tps = tpp.tile([P, P], F32, name="tps", tag="tp")
-        nc.tensor.transpose(tps[:], srow[:], ident_f[:])
-        scale_col = const.tile([P, 16], F32, name="scale_col")
-        nc.vector.tensor_copy(out=scale_col[:], in_=tps[:, 0:16])
         for q in range(4):
             psb = accp.tile([P, 4, P], F32, name="psb", tag="acc")
             for c in range(4):
                 col = 4 * q + c
                 nc.tensor.transpose(psb[:, c, :], scale_col[:, col : col + 1].to_broadcast([P, P]), ident_f[:])
-            nc.scalar.copy(out=scale_bc[:, 512 * q : 512 * (q + 1)], in_=psb[:].rearrange("p c n -> p (c n)"))
+            nc.scalar.copy(
+                out=scale_bc[:, 512 * q : 512 * (q + 1)].rearrange("p (n c) -> p n c", c=4), in_=psb[:].rearrange("p c n -> p n c")
+            )
         ident_b = const.tile([P, P], BF16, name="ident_b")
         make_identity(nc, ident_b[:])
         swapm = const.tile([P, 64, 2], F32, name="swapm")

@@ -23,6 +23,7 @@ OUTW = HEADS * HW
 NCHUNK = 8
 NROW = 24
 NWARM = 3
+RX = 14
 
 FLOPS = 2 * TOK * K * 3072
 
@@ -70,6 +71,8 @@ def tile_lorentzmla_pb_kernel(tc, x, freqs_cos, freqs_sin, wq_w_bytes, wq_w_scal
         nc.sync.dma_start(
             out=scale_col[:].rearrange("p (g t) -> p g t", t=4), in_=scale_row.rearrange("(g p t) -> p g t", p=P, t=4)
         )
+        wbx = const.tile([P, K], U8, name="wbx")
+        nc.sync.dma_start(out=wbx[:], in_=w_v[:, RX, :])
         load_w_row(0, 0)
         load_w_row(0, 1)
         load_w_row(0, 2)
@@ -82,7 +85,10 @@ def tile_lorentzmla_pb_kernel(tc, x, freqs_cos, freqs_sin, wq_w_bytes, wq_w_scal
         load_w_row(1, 2)
         for a in range(2, NCHUNK):
             new_w(a)
-            nc.sync.dma_start(out=wbytes[a][:], in_=w_v[:, 3 * a : 3 * a + 3, :])
+            nrow = 2 if a == RX // 3 else 3
+            nc.sync.dma_start(out=wbytes[a][:, 0:nrow, :], in_=w_v[:, 3 * a : 3 * a + nrow, :])
+        wcast = const.tile([P, K], BF16, name="wcast")
+        nc.vector.tensor_copy(out=wcast[:], in_=wbx[:].bitcast(FP8))
 
         cos_raw = const.tile([P, 2, 64], BF16, name="cos_raw")
         sin_raw = const.tile([P, 2, 64], BF16, name="sin_raw")
@@ -209,6 +215,18 @@ def tile_lorentzmla_pb_kernel(tc, x, freqs_cos, freqs_sin, wq_w_bytes, wq_w_scal
                 in_=wg[(a, grp)][:].rearrange("p g n c t -> p (g n c t)"),
             )
             wc[(a, grp)] = (cod, sca)
+
+        wgx = const.tile([P, PASSES, 1, P, 4], BF16, name="wgx", align_bytes=64)
+        wg[(RX // 3, 1)] = wgx
+        wraw = const.tile([P, PASSES, 1, P, 4], BF16, name="wraw")
+
+        def wtx_half(gp):
+            tp = word_transposes(wcast, gp, ident_f[:])
+            nc.scalar.copy(out=wraw[:].bitcast(F32)[:, 2 * gp : 2 * gp + 2, 0, :, :], in_=tp[:].rearrange("p u g r -> p g r u"))
+
+        def scale_x(col):
+            g, t = divmod(col, 4)
+            nc.scalar.activation(out=wgx[:, g, 0, :, t], in_=wraw[:, g, 0, :, t], func=ACT.Copy, scale=scale_col[:, col : col + 1])
 
         def unit_info(t):
             a, i = divmod(t, 3)
@@ -344,6 +362,8 @@ def tile_lorentzmla_pb_kernel(tc, x, freqs_cos, freqs_sin, wq_w_bytes, wq_w_scal
                 return None
             return (a, j - 1)
 
+        wtx_half(0)
+        wtx_half(1)
         x_at = {1: (0,), 2: (1,), 3: (2, 3)}
         for s in range(NROW + 6 + 1):
             t = s - 5
@@ -357,14 +377,17 @@ def tile_lorentzmla_pb_kernel(tc, x, freqs_cos, freqs_sin, wq_w_bytes, wq_w_scal
                 st_quant(g[0], g[1])
             if s == 4:
                 x_quant()
-            if s < NROW:
+            if s < NROW and s != RX:
                 st_tt(s)
             for half in range(2):
                 if 0 <= s - 4 < NROW:
                     mx_half(s - 4, half)
             for half in range(2):
-                if 0 <= s - 1 < NROW:
+                if 0 <= s - 1 < NROW and s - 1 != RX:
                     wt_half(s - 1, half)
+            if 5 <= s < 13:
+                scale_x(2 * (s - 5))
+                scale_x(2 * (s - 5) + 1)
             for half in range(2):
                 if 0 <= s - 6 < NROW:
                     back_half(s - 6, half)

@@ -125,12 +125,12 @@ def tile_lorentzmla_pb_kernel(tc, x, freqs_cos, freqs_sin, wq_w_bytes, wq_w_scal
         make_identity(nc, ident_b[:])
         swapm = const.tile([P, 64, 2], F32, name="swapm")
         idv = ident_f[:].rearrange("p (j e) -> p j e", e=2)
-        nc.scalar.copy(out=swapm[:, :, 0], in_=idv[:, :, 1])
-        nc.scalar.copy(out=swapm[:, :, 1], in_=idv[:, :, 0])
+        nc.vector.tensor_copy(out=swapm[:, :, 0], in_=idv[:, :, 1])
+        nc.vector.tensor_copy(out=swapm[:, :, 1], in_=idv[:, :, 0])
         swap2 = swapm[:].rearrange("p j e -> p (j e)")
         rot64 = const.tile([P, P], F32, name="rot64")
-        nc.scalar.copy(out=rot64[:, 0:64], in_=ident_f[:, 64:128])
-        nc.scalar.copy(out=rot64[:, 64:128], in_=ident_f[:, 0:64])
+        nc.vector.tensor_copy(out=rot64[:, 0:64], in_=ident_f[:, 64:128])
+        nc.vector.tensor_copy(out=rot64[:, 64:128], in_=ident_f[:, 0:64])
 
         c_il = const.tile([P, 2, 64, 2], BF16, name="c_il")
         s_il = const.tile([P, 2, 64, 2], BF16, name="s_il")

@@ -134,10 +134,10 @@ def tile_lorentzmla_pb_kernel(tc, x, freqs_cos, freqs_sin, wq_w_bytes, wq_w_scal
 
         c_il = const.tile([P, 2, 64, 2], BF16, name="c_il")
         s_il = const.tile([P, 2, 64, 2], BF16, name="s_il")
-        nc.scalar.copy(out=c_il[:, :, :, 0], in_=cos_raw[:])
-        nc.scalar.copy(out=c_il[:, :, :, 1], in_=cos_raw[:])
-        nc.scalar.copy(out=s_il[:, :, :, 0], in_=sin_raw[:])
-        nc.scalar.mul(out=s_il[:, :, :, 1], in_=sin_raw[:], mul=-1.0)
+        nc.vector.tensor_copy(out=c_il[:, :, :, 0], in_=cos_raw[:])
+        nc.vector.tensor_copy(out=c_il[:, :, :, 1], in_=cos_raw[:])
+        nc.vector.tensor_copy(out=s_il[:, :, :, 0], in_=sin_raw[:])
+        nc.vector.tensor_scalar(out=s_il[:, :, :, 1], in0=sin_raw[:], scalar1=-1.0, scalar2=None, op0=ALU.mult)
 
         tpt = tpp.tile([P, 4, P], BF16, name="tpt", tag="tp")
         for st in range(2):

from contextlib import ExitStack

import concourse.mybir as mybir
from concourse.masks import make_identity

F32 = mybir.dt.float32
BF16 = mybir.dt.bfloat16
U32 = mybir.dt.uint32
U8 = mybir.dt.uint8
FP8 = mybir.dt.float8_e4m3fn
FP8X4 = mybir.dt.float8_e4m3fn_x4
ALU = mybir.AluOpType
ACT = mybir.ActivationFunctionType

P = 128
K = 2048
PASSES = 4
TOK = 512
MT = 4
HEADS = 16
HW = 193
OUTW = HEADS * HW
NCHUNK = 8
NROW = 24
NWARM = 3
RX = 14

FLOPS = 2 * TOK * K * 3072


def tile_lorentzmla_pb_kernel(tc, x, freqs_cos, freqs_sin, wq_w_bytes, wq_w_scale, wq_b, out):
    nc = tc.nc
    x_v = x.flatten_outer_dims()
    w_v = wq_w_bytes.rearrange("(i p) k -> p i k", p=P)
    out_v = out.rearrange("b (st p) h c -> p (b st) (h c)", p=P)
    scale_row = wq_w_scale.rearrange("o k -> (o k)")

    with ExitStack() as ctx:
        const = ctx.enter_context(tc.tile_pool(name="const", bufs=1))
        wbp = ctx.enter_context(tc.tile_pool(name="wbp", bufs=6))
        xsp = ctx.enter_context(tc.tile_pool(name="xsp", bufs=4))
        wbfp = ctx.enter_context(tc.tile_pool(name="wbfp", bufs=4))
        wgp = ctx.enter_context(tc.tile_pool(name="wgp", bufs=2))
        wcp = ctx.enter_context(tc.tile_pool(name="wcp", bufs=2))
        up = ctx.enter_context(tc.tile_pool(name="up", bufs=4))
        qnp = ctx.enter_context(tc.tile_pool(name="qnp", bufs=2))
        tpp = ctx.enter_context(tc.psum_pool(name="tpp", bufs=3))
        accp = ctx.enter_context(tc.psum_pool(name="accp", bufs=3))
        finp = ctx.enter_context(tc.psum_pool(name="finp", bufs=2))
        ctx.enter_context(tc.manual_schedule(engines={mybir.EngineType.PE}))

        scale_bc = const.tile([P, K], F32, name="scale_bc")
        wbytes = {}
        xs = {}

        def new_w(a):
            wbytes[a] = wbp.tile([P, 3, K], U8, name="wbytes", tag="wbytes")

        def load_w_row(a, j):
            nc.sync.dma_start(out=wbytes[a][:, j, :], in_=w_v[:, 3 * a + j, :])

        def load_x(m):
            xs[m] = xsp.tile([P, K], BF16, name="xs", tag="xs")
            nc.sync.dma_start(out=xs[m][:], in_=x_v[m * P : (m + 1) * P, :])

        new_w(0)
        new_w(1)
        scale_col = const.tile([P, 16], F32, name="scale_col")
        wones = const.tile([P, 512], BF16, name="wones")
        nc.gpsimd.memset(wones[:], 1.0)
        nc.sync.dma_start(
            out=scale_col[:].rearrange("p (g t) -> p g t", t=4), in_=scale_row.rearrange("(g p t) -> p g t", p=P, t=4)
        )
        wbx = const.tile([P, K], U8, name="wbx")
        nc.sync.dma_start(out=wbx[:], in_=w_v[:, RX, :])
        load_w_row(0, 0)
        load_w_row(0, 1)
        load_w_row(0, 2)
        load_x(0)
        load_x(1)
        load_w_row(1, 0)
        load_x(2)
        load_w_row(1, 1)
        load_x(3)
        load_w_row(1, 2)
        for a in range(2, NCHUNK):
            new_w(a)
            nrow = 2 if a == RX // 3 else 3
            nc.sync.dma_start(out=wbytes[a][:, 0:nrow, :], in_=w_v[:, 3 * a : 3 * a + nrow, :])
        wcast = const.tile([P, K], BF16, name="wcast")
        nc.vector.tensor_copy(out=wcast[:], in_=wbx[:].bitcast(FP8))

        cos_raw = const.tile([P, 2, 64], BF16, name="cos_raw")
        sin_raw = const.tile([P, 2, 64], BF16, name="sin_raw")
        nc.scalar.dma_start(out=cos_raw[:], in_=freqs_cos.rearrange("(st p) j -> p st j", p=P))
        nc.scalar.dma_start(out=sin_raw[:], in_=freqs_sin.rearrange("(st p) j -> p st j", p=P))
        braw = const.tile([P, P], BF16, name="braw")
        nc.gpsimd.memset(braw[:], 0.0)
        warm = const.tile([P, 1], F32, name="warm")
        nc.gpsimd.memset(warm[:], 1.0)
        nc.scalar.dma_start(out=braw[0:16, :], in_=wq_b.rearrange("(h c) -> h c", c=192)[:, 64:192])
        nc.scalar.dma_start(
            out=braw[16:24, :].rearrange("a (f c) -> a f c", f=2),
            in_=wq_b.rearrange("(a f c) -> a f c", f=2, c=192)[:, :, 0:64],
        )

        for i in range(NWARM):
            wps = finp.tile([P, 512], F32, name="wps", tag="fin")
            nc.tensor.matmul(wps[:], lhsT=wones[:, 0:P], rhs=wones[:], start=True, stop=True)

        warm2 = const.tile([P, 1], F32, name="warm2")
        nc.scalar.activation(out=warm2[:], in_=warm[:], func=ACT.Sqrt)

        ident_f = const.tile([P, P], F32, name="ident_f")
        make_identity(nc, ident_f[:])
        for q in range(4):
            psb = accp.tile([P, 4, P], F32, name="psb", tag="acc")
            for c in range(4):
                col = 4 * q + c
                nc.tensor.transpose(psb[:, c, :], scale_col[:, col : col + 1].to_broadcast([P, P]), ident_f[:])
            nc.scalar.copy(
                out=scale_bc[:, 512 * q : 512 * (q + 1)].rearrange("p (n c) -> p n c", c=4), in_=psb[:].rearrange("p c n -> p n c")
            )
        ident_b = const.tile([P, P], BF16, name="ident_b")
        make_identity(nc, ident_b[:])
        swapm = const.tile([P, 64, 2], F32, name="swapm")
        idv = ident_f[:].rearrange("p (j e) -> p j e", e=2)
        nc.vector.tensor_copy(out=swapm[:, :, 0], in_=idv[:, :, 1])
        nc.vector.tensor_copy(out=swapm[:, :, 1], in_=idv[:, :, 0])
        swap2 = swapm[:].rearrange("p j e -> p (j e)")
        rot64 = const.tile([P, P], F32, name="rot64")
        nc.vector.tensor_copy(out=rot64[:, 0:64], in_=ident_f[:, 64:128])
        nc.vector.tensor_copy(out=rot64[:, 64:128], in_=ident_f[:, 0:64])

        c_il = const.tile([P, 2, 64, 2], BF16, name="c_il")
        s_il = const.tile([P, 2, 64, 2], BF16, name="s_il")
        nc.vector.tensor_copy(out=c_il[:, :, :, 0], in_=cos_raw[:])
        nc.vector.tensor_copy(out=c_il[:, :, :, 1], in_=cos_raw[:])
        nc.vector.tensor_copy(out=s_il[:, :, :, 0], in_=sin_raw[:])
        nc.vector.tensor_scalar(out=s_il[:, :, :, 1], in0=sin_raw[:], scalar1=-1.0, scalar2=None, op0=ALU.mult)

        tpt = tpp.tile([P, 4, P], BF16, name="tpt", tag="tp")
        for st in range(2):
            nc.tensor.transpose(tpt[:, st, :], c_il[:, st, :, :].rearrange("p j e -> p (j e)"), ident_b[:])
            nc.tensor.transpose(tpt[:, 2 + st, :], s_il[:, st, :, :].rearrange("p j e -> p (j e)"), ident_b[:])
        cs_t = const.tile([P, 2, 2, 256], F32, name="cs_t")
        for b in range(2):
            nc.scalar.copy(out=cs_t[:, 0, b, :], in_=tpt[:, 0:2, :].rearrange("p s r -> p (s r)"))
            nc.scalar.copy(out=cs_t[:, 1, b, :], in_=tpt[:, 2:4, :].rearrange("p s r -> p (s r)"))
        cs_f = cs_t[:].rearrange("p k b s -> p k (b s)")

        tpb = tpp.tile([P, P], BF16, name="tpb", tag="tp")
        nc.tensor.transpose(tpb[:], braw[:], ident_b[:])
        bias_col = const.tile([P, 24], F32, name="bias_col")
        nc.scalar.copy(out=bias_col[:], in_=tpb[:, 0:24])

        x_codes = const.tile([P, PASSES, TOK], U32, name="x_codes", align_bytes=64)
        x_scales = const.tile([P, PASSES, TOK], U8, name="x_scales", align_bytes=64)
        xg = const.tile([P, PASSES, TOK, 4], BF16, name="xg", align_bytes=64)
        o_sb = const.tile([P, MT, OUTW], F32, name="o_sb")
        o4 = o_sb[:].rearrange("p m (h c) -> p m h c", c=HW)
        ssum = const.tile([P, MT, HEADS], F32, name="ssum")

        def word_transposes(src, gp, perm):
            words = src[:].bitcast(F32)
            tp = tpp.tile([P, 2, 2, P], F32, name="tp", tag="tp")
            for g2 in range(2):
                g = 2 * gp + g2
                for u in range(2):
                    nc.tensor.transpose(tp[:, u, g2, :], words[:, 256 * g + u : 256 * (g + 1) : 2], perm)
            return tp

        wbf = {}
        wg = {}
        wc = {}
        acc = {}
        post = {}
        fins = {}

        def st_tt(r):
            a, j = divmod(r, 3)
            t = wbfp.tile([P, K], BF16, name="wbf", tag="wbf")
            pieces = 4 if r == 0 else 1
            w = K // pieces
            for q in range(pieces):
                qs = slice(q * w, (q + 1) * w)
                nc.vector.tensor_tensor(out=t[:, qs], in0=wbytes[a][:, j, qs].bitcast(FP8), in1=scale_bc[:, qs], op=ALU.mult)
            wbf[r] = t

        def wt_half(r, gp):
            a, j = divmod(r, 3)
            if j == 0 and gp == 0:
                wg[(a, 0)] = wgp.tile([P, PASSES, 2, P, 4], BF16, name="wga", tag="wga", align_bytes=64)
            if j == 2 and gp == 0:
                wg[(a, 1)] = wgp.tile([P, PASSES, 1, P, 4], BF16, name="wgb", tag="wgb", align_bytes=64)
            tp = word_transposes(wbf[r], gp, rot64[:] if j == 1 else ident_f[:])
            gs = slice(2 * gp, 2 * gp + 2)
            if j == 2:
                dst = wg[(a, 1)][:].bitcast(F32)
                nc.scalar.copy(out=dst[:, gs, 0, :, :], in_=tp[:].rearrange("p u g r -> p g r u"))
            else:
                dst = wg[(a, 0)][:].bitcast(F32).rearrange("p g n c u -> p (g n) c u")
                nc.scalar.copy(
                    out=dst[:, 4 * gp : 4 * gp + 4, 64 * j : 64 * j + 64, :],
                    in_=tp[:].rearrange("p u g (n r) -> p (g n) r u", n=2),
                )

        def st_quant(a, grp):
            n = 2 if grp == 0 else 1
            cod = wcp.tile([P, PASSES, n, P], U32, name="wcod%d" % grp, tag="wcod%d" % grp, align_bytes=64)
            sca = wcp.tile([P, PASSES, n, P], U8, name="wsca%d" % grp, tag="wsca%d" % grp, align_bytes=64)
            nc.vector.quantize_mx(
                out=cod[:].rearrange("p g n c -> p (g n c)").bitcast(FP8X4),
                scales=sca[:].rearrange("p g n c -> p (g n c)"),
                in_=wg[(a, grp)][:].rearrange("p g n c t -> p (g n c t)"),
            )
            wc[(a, grp)] = (cod, sca)

        wgx = const.tile([P, PASSES, 1, P, 4], BF16, name="wgx", align_bytes=64)
        wg[(RX // 3, 1)] = wgx
        wraw = const.tile([P, PASSES, 1, P, 4], BF16, name="wraw")

        def wtx_half(gp):
            tp = word_transposes(wcast, gp, ident_f[:])
            nc.scalar.copy(out=wraw[:].bitcast(F32)[:, 2 * gp : 2 * gp + 2, 0, :, :], in_=tp[:].rearrange("p u g r -> p g r u"))

        def scale_x(col):
            g, t = divmod(col, 4)
            nc.scalar.activation(out=wgx[:, g, 0, :, t], in_=wraw[:, g, 0, :, t], func=ACT.Copy, scale=scale_col[:, col : col + 1])

        def unit_info(t):
            a, i = divmod(t, 3)
            if i == 0:
                return (False, a, 0, 0, 16 + a)
            if i == 1:
                return (True, 2 * a, 0, 1, 2 * a)
            return (True, 2 * a + 1, 1, 0, 2 * a + 1)

        def mx_half(t, half):
            rot, idx, grp, n, bcol = unit_info(t)
            cod, sca = wc[(t // 3, grp)]
            if half == 0:
                acc[t] = accp.tile([P, TOK], F32, name="acc", tag="acc")
            for g in (2 * half, 2 * half + 1):
                nc.tensor.matmul_mx(
                    out=acc[t][:],
                    lhsT=cod[:, g, n, :].bitcast(FP8X4),
                    lhsT_scale=sca[:, g, n, :],
                    rhs=x_codes[:, g, :].bitcast(FP8X4),
                    rhs_scale=x_scales[:, g, :],
                    start=(g == 0),
                    stop=(g == PASSES - 1),
                )

        def st_post(t):
            rot, idx, grp, n, bcol = unit_info(t)
            b_ap = bias_col[:, bcol : bcol + 1]
            if rot:
                u = up.tile([P, 2, TOK], F32, name="u", tag="u")
                pieces = MT if t == NROW - 1 else 1
                w = TOK // pieces
                for q in range(pieces):
                    qs = slice(q * w, (q + 1) * w)
                    nc.vector.scalar_tensor_tensor(
                        out=u[:, :, qs],
                        in0=acc[t][:, qs].unsqueeze(1).to_broadcast([P, 2, w]),
                        scalar=b_ap,
                        in1=cs_f[:, :, qs],
                        op0=ALU.add,
                        op1=ALU.mult,
                    )
                post[t] = (u[:, 0, :], u[:, 1, :])
            else:
                qn = qnp.tile([P, TOK], F32, name="qn", tag="qn")
                nc.scalar.activation(out=qn[:], in_=acc[t][:], func=ACT.Identity, bias=b_ap, scale=1.0)
                post[t] = (qn[:],)

        def back_last(t):
            rot, idx, grp, n, bcol = unit_info(t)
            src = post[t]
            for m in range(MT):
                ms = slice(m * P, (m + 1) * P)
                finq = tpp.tile([P, P], F32, name="finq", tag="tp")
                nc.tensor.matmul(finq[:], lhsT=src[0][:, ms], rhs=ident_f[:], is_transpose=True, start=True, stop=False)
                nc.tensor.matmul(finq[:], lhsT=src[1][:, ms], rhs=swap2, is_transpose=True, start=False, stop=True)
                nc.scalar.copy(out=o4[:, m, idx, 65:193], in_=finq[:])

        def back_half(t, half):
            rot, idx, grp, n, bcol = unit_info(t)
            if t == NROW - 1:
                if half == 0:
                    back_last(t)
                return
            if half == 0:
                fins[t] = finp.tile([P, MT, P], F32, name="fin", tag="fin")
            fin = fins[t]
            src = post[t]
            for m in (2 * half, 2 * half + 1):
                ms = slice(m * P, (m + 1) * P)
                if rot:
                    nc.tensor.matmul(fin[:, m, :], lhsT=src[0][:, ms], rhs=ident_f[:], is_transpose=True, start=True, stop=False)
                    nc.tensor.matmul(fin[:, m, :], lhsT=src[1][:, ms], rhs=swap2, is_transpose=True, start=False, stop=True)
                else:
                    nc.tensor.transpose(fin[:, m, :], src[0][:, ms], ident_f[:])
            if half == 1:
                if rot:
                    nc.scalar.copy(out=o4[:, :, idx, 65:193], in_=fin[:])
                else:
                    nc.scalar.copy(
                        out=o4[:, :, 2 * idx : 2 * idx + 2, 1:65],
                        in_=fin[:].rearrange("p m (f c) -> p m f c", f=2),
                    )

        def squares(h, on_vector):
            for m in range(MT):
                q_ap = o4[:, m, h, 1:193]
                s_ap = ssum[:, m, h : h + 1]
                if m in on_vector:
                    junkv = qnp.tile([P, 192], F32, name="junkv", tag="junkv")
                    nc.vector.scalar_tensor_tensor(out=junkv[:], in0=q_ap, scalar=1.0, in1=q_ap, op0=ALU.mult, op1=ALU.mult, accum_out=s_ap)
                else:
                    junk = qnp.tile([P, 192], F32, name="junk", tag="junk")
                    nc.scalar.activation(out=junk[:], in_=q_ap, func=ACT.Square, accum_out=s_ap)

        def finish(h0, h1):
            nc.scalar.activation(out=o4[:, :, h0:h1, 0], in_=ssum[:, :, h0:h1], func=ACT.Sqrt, bias=1.0, scale=1.0)
            c0 = (h0 * HW) // 8 * 8
            c1 = (h1 * HW) // 8 * 8
            nc.sync.dma_start(out=out_v[:, :, c0:c1], in_=o_sb[:, :, c0:c1])

        def st_tail(t):
            rot, h, grp, n, bcol = unit_info(t)
            if not rot:
                return
            last = t // 3 == NCHUNK - 1
            squares(h, (0, 1, 2) if t == NROW - 1 else ())
            if last:
                finish(h, h + 1)
            elif grp == 1:
                finish(h - 1, h + 1)

        def x_transposes(m):
            xgw = xg[:].bitcast(F32)
            for gp in range(2):
                tp = word_transposes(xs[m], gp, ident_f[:])
                nc.scalar.copy(
                    out=xgw[:, 2 * gp : 2 * gp + 2, m * P : (m + 1) * P, :],
                    in_=tp[:].rearrange("p u g r -> p g r u"),
                )

        def x_quant():
            for g in range(PASSES):
                nc.vector.quantize_mx(
                    out=x_codes[:, g, :].bitcast(FP8X4),
                    scales=x_scales[:, g, :],
                    in_=xg[:, g, :, :].rearrange("p n t -> p (n t)"),
                )

        def group_of(r):
            a, j = divmod(r, 3)
            if r < 0 or r >= NROW or j == 0:
                return None
            return (a, j - 1)

        wtx_half(0)
        wtx_half(1)
        x_at = {1: (0,), 2: (1,), 3: (2, 3)}
        for s in range(NROW + 6 + 1):
            t = s - 5
            if 0 <= t < NROW and unit_info(t)[0]:
                st_post(t)
            t = s - 5
            if 0 <= t < NROW and not unit_info(t)[0]:
                st_post(t)
            g = group_of(s - 2)
            if g is not None:
                st_quant(g[0], g[1])
            if s == 4:
                x_quant()
            if s < NROW and s != RX:
                st_tt(s)
            for half in range(2):
                if 0 <= s - 4 < NROW:
                    mx_half(s - 4, half)
            for half in range(2):
                if 0 <= s - 1 < NROW and s - 1 != RX:
                    wt_half(s - 1, half)
            if 5 <= s < 13:
                scale_x(2 * (s - 5))
                scale_x(2 * (s - 5) + 1)
            for half in range(2):
                if 0 <= s - 6 < NROW:
                    back_half(s - 6, half)
            for m in x_at.get(s, ()):
                x_transposes(m)
            if 0 <= s - 6 < NROW:
                st_tail(s - 6)
